import numpy as np
import ml_dtypes


def mxq(x, axis, fmt="e4m3"):
    dtype, down = {"e4m3": (ml_dtypes.float8_e4m3fn, 7), "e5m2": (ml_dtypes.float8_e5m2, 14)}[fmt]
    v = np.moveaxis(np.asarray(x, np.float32).astype(ml_dtypes.bfloat16).astype(np.float64), axis, -1)
    blocks = v.reshape(v.shape[:-1] + (-1, 32))
    amax = np.abs(blocks).max(-1, keepdims=True)
    byte = np.maximum(np.where(amax > 0, np.frexp(amax)[1] - 1 + 127, 0) - down, 1)
    scale = np.exp2(byte - 127.0)
    codes = (blocks / scale).astype(np.float32).astype(dtype).astype(np.float64)
    return np.moveaxis((codes * scale).reshape(v.shape), -1, axis)


WIDE = False


def mx_kscale(k):
    if not WIDE:
        return np.ones(k)
    levels = np.array([10, -10, 5, -5, 0])
    a = np.random.permutation(np.resize(levels, k // 512 * 4)).reshape(k // 512, 4)
    idx = np.arange(k)
    return np.exp2(a[idx // 512, idx % 128 // 32])


BF16 = ml_dtypes.bfloat16


def bf(x):
    return np.asarray(x, np.float32).astype(BF16)


def f64(x):
    return np.asarray(x).astype(np.float64)


B, N, VD, QD, D, H, NG, P = 32, 36, 2048, 1024, 1024, 8, 20, 64
DH = D // H


def setup_inputs():
    s = mx_kscale(D)
    return {"out_t": bf(np.random.standard_normal((B, N, H, D)) * 0.7 * s),
            "out_w": bf(np.random.standard_normal((H, D, DH)) / np.sqrt(D) / s[None, :, None]),
            "out_b": bf(np.random.standard_normal(D) * 0.3),
            "self_feat": bf(np.random.standard_normal((B, N, D)) * 0.9),
            "vis": bf(np.maximum(np.random.standard_normal((B, N, D)), 0.0))}


def reference(out_t, out_w, out_b, self_feat, vis):
    t = mxq(f64(out_t), 3, "e4m3").reshape(B * N, H, D).swapaxes(0, 1)
    nb = t @ mxq(f64(out_w), 1, "e4m3")
    neighbor = nb.swapaxes(0, 1).reshape(B, N, D) + f64(out_b)
    imp_rel = np.maximum(f64(self_feat) + neighbor, 0.0)
    return f64(vis) + imp_rel

@@ -1,0 +1,217 @@
+from contextlib import ExitStack
+
+import concourse.mybir as mybir
+from concourse.masks import make_identity
+
+BF16 = mybir.dt.bfloat16
+F32 = mybir.dt.float32
+U32 = mybir.dt.uint32
+U8 = mybir.dt.uint8
+FP8X4 = mybir.dt.float8_e4m3fn_x4
+ADD = mybir.AluOpType.add
+MAX = mybir.AluOpType.max
+
+P = 128
+ROWS = 32 * 36
+T = ROWS // P
+H = 8
+K = 1024
+DH = 128
+D = H * DH
+NCH = 2 * T
+NB = 4 * NCH
+
+FLOPS = 2 * ROWS * H * K * DH
+
+
+def tile_implicitrelationencoder_pb_kernel(tc, out_t, out_w, out_b, self_feat, vis, out):
+    nc = tc.nc
+    x_v = out_t.rearrange("b n h k -> (b n) (h k)").rearrange("(p t) f -> p t f", t=T)
+    w_v = out_w.rearrange("h (s q e) c -> q (h s) (e c)", q=P, e=2)
+    s_v = self_feat.rearrange("b n d -> (b n) d").rearrange("(p t) d -> p t d", t=T)
+    v_v = vis.rearrange("b n d -> (b n) d").rearrange("(p t) d -> p t d", t=T)
+    o_v = out.rearrange("b n d -> (b n) d").rearrange("(p t) d -> p t d", t=T)
+
+    with ExitStack() as ctx:
+        const = ctx.enter_context(tc.tile_pool(name="const", bufs=1))
+        xpool = ctx.enter_context(tc.tile_pool(name="xpool", bufs=6))
+        gpool = ctx.enter_context(tc.tile_pool(name="gpool", bufs=3))
+        cpool = ctx.enter_context(tc.tile_pool(name="cpool", bufs=3))
+        tpp = ctx.enter_context(tc.psum_pool(name="tpp", bufs=6))
+        accp = ctx.enter_context(tc.psum_pool(name="accp", bufs=2))
+        ctx.enter_context(tc.manual_schedule())
+
+        brow = const.tile([P, D], BF16)
+        ones = const.tile([P, P], BF16)
+        ident = const.tile([P, P], F32)
+        bias_bc = const.tile([P, D], F32)
+        wcodes = const.tile([P, 2 * H * DH], U32, align_bytes=64)
+        wscl = const.tile([P, 2 * H * DH], U8, align_bytes=64)
+        self_sb = [const.tile([P, 3, D], BF16, name="self%d" % i) for i in range(3)]
+        vis_sb = [const.tile([P, 3, D], BF16, name="vis%d" % i) for i in range(3)]
+        res = [const.tile([P, 3, D], F32, name="res%d" % i) for i in range(3)]
+
+        nc.gpsimd.memset(brow[:], 0.0)
+        nc.gpsimd.memset(ones[:], 1.0)
+        make_identity(nc, ident[:])
+
+        wraw = xpool.tile([P, 2 * 4096], BF16, tag="x")
+        xt = {}
+
+        def load_w(a):
+            nc.sync.dma_start(
+                out=wraw[:, 4096 * a : 4096 * (a + 1)].rearrange("p (b f) -> p b f", f=256),
+                in_=w_v[:, 16 * a : 16 * (a + 1), :],
+            )
+
+        def load_self(i):
+            nc.sync.dma_start(out=self_sb[i][:], in_=s_v[:, 3 * i : 3 * i + 3, :])
+
+        def load_vis(i):
+            nc.sync.dma_start(out=vis_sb[i][:], in_=v_v[:, 3 * i : 3 * i + 3, :])
+
+        def load_x(t, pieces):
+            xtile = xpool.tile([P, H * K], BF16, tag="x")
+            xt[t] = xtile
+            step = H * K // pieces
+            for i in range(pieces):
+                nc.sync.dma_start(
+                    out=xtile[:, step * i : step * (i + 1)], in_=x_v[:, t, step * i : step * (i + 1)]
+                )
+
+        load_w(0)
+        nc.sync.dma_start(out=brow[0:1, :], in_=out_b.rearrange("(o d) -> o d", o=1))
+        load_self(0)
+        load_w(1)
+        load_self(1)
+        load_self(2)
+        load_x(0, 2)
+        load_vis(0)
+        load_x(1, 1)
+        load_x(2, 1)
+        load_x(3, 1)
+        load_vis(1)
+        load_x(4, 1)
+
+        for i in range(2):
+            bp = tpp.tile([P, 512], F32, tag="tp")
+            nc.tensor.matmul(bp[:], lhsT=ones[:], rhs=brow[:, 512 * i : 512 * (i + 1)], start=True, stop=True)
+            nc.vector.tensor_copy(out=bias_bc[:, 512 * i : 512 * (i + 1)], in_=bp[:])
+
+        def e0(t):
+            nc.vector.tensor_tensor(
+                out=res[t // 3][:, t % 3, :], in0=self_sb[t // 3][:, t % 3, :], in1=bias_bc[:], op=ADD
+            )
+
+        def prep_w(a):
+            wg = gpool.tile([P, 4096], BF16, tag="g", align_bytes=64)
+            for b in range(8):
+                nc.scalar.copy(
+                    out=wg[:, 512 * b : 512 * (b + 1)].rearrange("p (c i t) -> p c t i", i=4, t=4),
+                    in_=wraw[:, 4096 * a + 512 * b : 4096 * a + 512 * (b + 1)].rearrange(
+                        "p (t c i) -> p c t i", t=4, i=4
+                    ),
+                )
+            return wg
+
+        def quant_w(a, wg):
+            nc.vector.quantize_mx(
+                out=wcodes[:, 1024 * a : 1024 * (a + 1)].bitcast(FP8X4),
+                scales=wscl[:, 1024 * a : 1024 * (a + 1)],
+                in_=wg[:],
+            )
+
+        wg0 = prep_w(0)
+        wg1 = prep_w(1)
+        for t in range(3):
+            e0(t)
+        quant_w(0, wg0)
+        for t in range(3, 6):
+            e0(t)
+        quant_w(1, wg1)
+        for t in range(6, 9):
+            e0(t)
+
+        tps = {}
+        gts = {}
+        cds = {}
+        accs = {}
+
+        def tb(n):
+            xw = xt[n // 8][:].bitcast(F32)
+            hh = n % 8
+            tp = tpp.tile([P, 4, P], F32, tag="tp")
+            tps[n] = tp
+            for u in range(4):
+                nc.tensor.transpose(tp[:, u, :], xw[:, 512 * hh + 128 * u : 512 * hh + 128 * (u + 1)], ident[:])
+
+        def cp(n):
+            c = n // 4
+            j = n % 4
+            if j == 0:
+                g = gpool.tile([P, 4096], BF16, tag="g", align_bytes=64)
+                gts[c] = g
+            gw = gts[c][:].bitcast(F32)
+            nc.scalar.copy(
+                out=gw[:, 512 * j : 512 * (j + 1)].rearrange("p (g r u) -> p g r u", g=2, u=2),
+                in_=tps[n][:].rearrange("p (g u) r -> p g r u", u=2),
+            )
+
+        def quant(c):
+            codes = cpool.tile([P, 1024], U32, tag="codes", align_bytes=64)
+            scl = cpool.tile([P, 1024], U8, tag="scl", align_bytes=64)
+            cds[c] = (codes, scl)
+            nc.vector.quantize_mx(out=codes[:].bitcast(FP8X4), scales=scl[:], in_=gts[c][:])
+
+        def mx(c):
+            codes, scl = cds[c]
+            acc = accp.tile([P, 512], F32, tag="acc")
+            accs[c] = acc
+            for j in range(4):
+                h = 4 * (c % 2) + j
+                for gp in range(2):
+                    xs = slice(256 * j + 128 * gp, 256 * j + 128 * (gp + 1))
+                    ws = slice(128 * (2 * h + gp), 128 * (2 * h + gp + 1))
+                    nc.tensor.matmul_mx(
+                        out=acc[:, 128 * j : 128 * (j + 1)],
+                        lhsT=codes[:, xs].bitcast(FP8X4),
+                        lhsT_scale=scl[:, xs],
+                        rhs=wcodes[:, ws].bitcast(FP8X4),
+                        rhs_scale=wscl[:, ws],
+                        start=(gp == 0),
+                        stop=(gp == 1),
+                    )
+
+        def epi(c):
+            t = c // 2
+            cols = slice(512 * (c % 2), 512 * (c % 2 + 1))
+            rs = res[t // 3][:, t % 3, cols]
+            nc.vector.tensor_tensor(out=rs, in0=accs[c][:], in1=rs, op=ADD)
+            nc.vector.scalar_tensor_tensor(
+                out=rs, in0=rs, scalar=0.0, in1=vis_sb[t // 3][:, t % 3, cols], op0=MAX, op1=ADD
+            )
+
+        for n in range(NB + 6):
+            if n < NB:
+                tb(n)
+                if n % 8 == 7:
+                    t = n // 8 + 5
+                    if t < T:
+                        load_x(t, 2 if t == T - 1 else 1)
+                        if t == 6:
+                            load_vis(2)
+            if n >= 5 and (n - 5) % 4 == 0 and 0 <= (n - 5) // 4 - 1 < NCH:
+                mx((n - 5) // 4 - 1)
+            if 0 <= n - 2 < NB:
+                cp(n - 2)
+            if n >= 5 and (n - 5) % 4 == 0:
+                c = (n - 5) // 4
+                if c < NCH:
+                    quant(c)
+                if 0 <= c - 1 < NCH:
+                    epi(c - 1)
+
+        nc.sync.dma_start(out=o_v[:, 0:3, :], in_=res[0][:])
+        nc.sync.dma_start(out=o_v[:, 3:6, :], in_=res[1][:])
+        nc.sync.dma_start(out=o_v[:, 6:8, :], in_=res[2][:, 0:2, :])
+        nc.sync.dma_start(out=o_v[:, 8, :], in_=res[2][:, 2, :])

@@ -96,7 +96,7 @@ def tile_implicitrelationencoder_pb_kernel(tc, out_t, out_w, out_b, self_feat, v
         for i in range(2):
             bp = tpp.tile([P, 512], F32, tag="tp")
             nc.tensor.matmul(bp[:], lhsT=ones[:], rhs=brow[:, 512 * i : 512 * (i + 1)], start=True, stop=True)
-            nc.vector.tensor_copy(out=bias_bc[:, 512 * i : 512 * (i + 1)], in_=bp[:])
+            nc.scalar.copy(out=bias_bc[:, 512 * i : 512 * (i + 1)], in_=bp[:])
 
         def e0(t):
             nc.vector.tensor_tensor(
@@ -182,11 +182,16 @@ def tile_implicitrelationencoder_pb_kernel(tc, out_t, out_w, out_b, self_feat, v
                         stop=(gp == 1),
                     )
 
-        def epi(c):
+        def epi1(c):
             t = c // 2
             cols = slice(512 * (c % 2), 512 * (c % 2 + 1))
             rs = res[t // 3][:, t % 3, cols]
             nc.vector.tensor_tensor(out=rs, in0=accs[c][:], in1=rs, op=ADD)
+
+        def epi2(c):
+            t = c // 2
+            cols = slice(512 * (c % 2), 512 * (c % 2 + 1))
+            rs = res[t // 3][:, t % 3, cols]
             nc.vector.scalar_tensor_tensor(
                 out=rs, in0=rs, scalar=0.0, in1=vis_sb[t // 3][:, t % 3, cols], op0=MAX, op1=ADD
             )
@@ -206,12 +211,15 @@ def tile_implicitrelationencoder_pb_kernel(tc, out_t, out_w, out_b, self_feat, v
                 cp(n - 2)
             if n >= 5 and (n - 5) % 4 == 0:
                 c = (n - 5) // 4
+                if 0 <= c - 1 < NCH:
+                    epi1(c - 1)
                 if c < NCH:
                     quant(c)
                 if 0 <= c - 1 < NCH:
-                    epi(c - 1)
+                    epi2(c - 1)
 
         nc.sync.dma_start(out=o_v[:, 0:3, :], in_=res[0][:])
         nc.sync.dma_start(out=o_v[:, 3:6, :], in_=res[1][:])
         nc.sync.dma_start(out=o_v[:, 6:8, :], in_=res[2][:, 0:2, :])
-        nc.sync.dma_start(out=o_v[:, 8, :], in_=res[2][:, 2, :])
+        nc.sync.dma_start(out=o_v[:, 8, 0:512], in_=res[2][:, 2, 0:512])
+        nc.sync.dma_start(out=o_v[:, 8, 512:1024], in_=res[2][:, 2, 512:1024])

@@ -18,8 +18,13 @@ H = 8
 K = 1024
 DH = 128
 D = H * DH
-NCH = 2 * T
-NB = 4 * NCH
+NB = T * H
+
+TP_BUFS = 6
+ACC_BUFS = 2
+G_BUFS = 3
+C_BUFS = 3
+X_BUFS = 6
 
 FLOPS = 2 * ROWS * H * K * DH
 
@@ -32,13 +37,33 @@ def tile_implicitrelationencoder_pb_kernel(tc, out_t, out_w, out_b, self_feat, v
     v_v = vis.rearrange("b n d -> (b n) d").rearrange("(p t) d -> p t d", t=T)
     o_v = out.rearrange("b n d -> (b n) d").rearrange("(p t) d -> p t d", t=T)
 
+    units = []
+    for t in range(T):
+        sizes = [2, 2, 2, 2] if t == T - 1 else [4, 4]
+        h0 = 0
+        for nh in sizes:
+            units.append((t, h0, nh))
+            h0 += nh
+    NU = len(units)
+    first_bank = [H * t + h0 for (t, h0, nh) in units]
+    last_bank = [H * t + h0 + nh - 1 for (t, h0, nh) in units]
+    unit_of_bank = {}
+    for i in range(NU):
+        for n in range(first_bank[i], last_bank[i] + 1):
+            unit_of_bank[n] = i
+
+    queues = {"sync": [], "pe": [], "act": [], "dve": []}
+
+    def op(queue, name, needs, emit):
+        queues[queue].append((name, [x for x in needs if x is not None], emit))
+
     with ExitStack() as ctx:
         const = ctx.enter_context(tc.tile_pool(name="const", bufs=1))
-        xpool = ctx.enter_context(tc.tile_pool(name="xpool", bufs=6))
-        gpool = ctx.enter_context(tc.tile_pool(name="gpool", bufs=3))
-        cpool = ctx.enter_context(tc.tile_pool(name="cpool", bufs=3))
-        tpp = ctx.enter_context(tc.psum_pool(name="tpp", bufs=6))
-        accp = ctx.enter_context(tc.psum_pool(name="accp", bufs=2))
+        xpool = ctx.enter_context(tc.tile_pool(name="xpool", bufs=X_BUFS))
+        gpool = ctx.enter_context(tc.tile_pool(name="gpool", bufs=G_BUFS))
+        cpool = ctx.enter_context(tc.tile_pool(name="cpool", bufs=C_BUFS))
+        tpp = ctx.enter_context(tc.psum_pool(name="tpp", bufs=TP_BUFS))
+        accp = ctx.enter_context(tc.psum_pool(name="accp", bufs=ACC_BUFS))
         ctx.enter_context(tc.manual_schedule())
 
         brow = const.tile([P, D], BF16)
@@ -55,14 +80,23 @@ def tile_implicitrelationencoder_pb_kernel(tc, out_t, out_w, out_b, self_feat, v
         nc.gpsimd.memset(ones[:], 1.0)
         make_identity(nc, ident[:])
 
-        wraw = xpool.tile([P, 2 * 4096], BF16, tag="x")
         xt = {}
+        tps = {}
+        gts = {}
+        cds = {}
+        accs = {}
 
         def load_w(a):
+            if a == 0:
+                wraw = xpool.tile([P, H * K], BF16, tag="x")
+                xt["w"] = wraw
             nc.sync.dma_start(
-                out=wraw[:, 4096 * a : 4096 * (a + 1)].rearrange("p (b f) -> p b f", f=256),
+                out=xt["w"][:, 4096 * a : 4096 * (a + 1)].rearrange("p (b f) -> p b f", f=256),
                 in_=w_v[:, 16 * a : 16 * (a + 1), :],
             )
+
+        def load_bias():
+            nc.sync.dma_start(out=brow[0:1, :], in_=out_b.rearrange("(o d) -> o d", o=1))
 
         def load_self(i):
             nc.sync.dma_start(out=self_sb[i][:], in_=s_v[:, 3 * i : 3 * i + 3, :])
@@ -70,105 +104,55 @@ def tile_implicitrelationencoder_pb_kernel(tc, out_t, out_w, out_b, self_feat, v
         def load_vis(i):
             nc.sync.dma_start(out=vis_sb[i][:], in_=v_v[:, 3 * i : 3 * i + 3, :])
 
-        def load_x(t, pieces):
-            xtile = xpool.tile([P, H * K], BF16, tag="x")
-            xt[t] = xtile
-            step = H * K // pieces
-            for i in range(pieces):
-                nc.sync.dma_start(
-                    out=xtile[:, step * i : step * (i + 1)], in_=x_v[:, t, step * i : step * (i + 1)]
-                )
+        def load_x(i):
+            t, h0, nh = units[i]
+            if h0 == 0:
+                xtile = xpool.tile([P, H * K], BF16, tag="x")
+                xt[t] = xtile
+            nc.sync.dma_start(out=xt[t][:, K * h0 : K * (h0 + nh)], in_=x_v[:, t, K * h0 : K * (h0 + nh)])
 
-        load_w(0)
-        nc.sync.dma_start(out=brow[0:1, :], in_=out_b.rearrange("(o d) -> o d", o=1))
-        load_self(0)
-        load_w(1)
-        load_self(1)
-        load_self(2)
-        load_x(0, 2)
-        load_vis(0)
-        load_x(1, 1)
-        load_x(2, 1)
-        load_x(3, 1)
-        load_vis(1)
-        load_x(4, 1)
+        def queue_x(t):
+            if t < X_BUFS - 1:
+                slot = None
+            elif t == X_BUFS - 1:
+                slot = "R15"
+            else:
+                slot = "TB%d" % (H * (t - X_BUFS) + H - 1)
+            for i in range(NU):
+                if units[i][0] == t:
+                    op("sync", "x%d" % i, [slot], lambda i=i: load_x(i))
 
-        for i in range(2):
+        op("sync", "w0", [], lambda: load_w(0))
+        op("sync", "bias", [], load_bias)
+        op("sync", "self0", [], lambda: load_self(0))
+        op("sync", "w1", [], lambda: load_w(1))
+        op("sync", "self1", [], lambda: load_self(1))
+        op("sync", "self2", [], lambda: load_self(2))
+        for t in range(T):
+            queue_x(t)
+            if t % 3 == 1:
+                op("sync", "vis%d" % (t // 3), [], lambda i=t // 3: load_vis(i))
+
+        def bias_mm(i):
             bp = tpp.tile([P, 512], F32, tag="tp")
+            tps["b%d" % i] = bp
             nc.tensor.matmul(bp[:], lhsT=ones[:], rhs=brow[:, 512 * i : 512 * (i + 1)], start=True, stop=True)
-            nc.scalar.copy(out=bias_bc[:, 512 * i : 512 * (i + 1)], in_=bp[:])
-
-        def e0(t):
-            nc.vector.tensor_tensor(
-                out=res[t // 3][:, t % 3, :], in0=self_sb[t // 3][:, t % 3, :], in1=bias_bc[:], op=ADD
-            )
-
-        def prep_w(a):
-            wg = gpool.tile([P, 4096], BF16, tag="g", align_bytes=64)
-            for b in range(8):
-                nc.scalar.copy(
-                    out=wg[:, 512 * b : 512 * (b + 1)].rearrange("p (c i t) -> p c t i", i=4, t=4),
-                    in_=wraw[:, 4096 * a + 512 * b : 4096 * a + 512 * (b + 1)].rearrange(
-                        "p (t c i) -> p c t i", t=4, i=4
-                    ),
-                )
-            return wg
-
-        def quant_w(a, wg):
-            nc.vector.quantize_mx(
-                out=wcodes[:, 1024 * a : 1024 * (a + 1)].bitcast(FP8X4),
-                scales=wscl[:, 1024 * a : 1024 * (a + 1)],
-                in_=wg[:],
-            )
-
-        wg0 = prep_w(0)
-        wg1 = prep_w(1)
-        for t in range(3):
-            e0(t)
-        quant_w(0, wg0)
-        for t in range(3, 6):
-            e0(t)
-        quant_w(1, wg1)
-        for t in range(6, 9):
-            e0(t)
-
-        tps = {}
-        gts = {}
-        cds = {}
-        accs = {}
 
         def tb(n):
-            xw = xt[n // 8][:].bitcast(F32)
-            hh = n % 8
+            xw = xt[n // H][:].bitcast(F32)
+            hh = n % H
             tp = tpp.tile([P, 4, P], F32, tag="tp")
             tps[n] = tp
             for u in range(4):
                 nc.tensor.transpose(tp[:, u, :], xw[:, 512 * hh + 128 * u : 512 * hh + 128 * (u + 1)], ident[:])
 
-        def cp(n):
-            c = n // 4
-            j = n % 4
-            if j == 0:
-                g = gpool.tile([P, 4096], BF16, tag="g", align_bytes=64)
-                gts[c] = g
-            gw = gts[c][:].bitcast(F32)
-            nc.scalar.copy(
-                out=gw[:, 512 * j : 512 * (j + 1)].rearrange("p (g r u) -> p g r u", g=2, u=2),
-                in_=tps[n][:].rearrange("p (g u) r -> p g r u", u=2),
-            )
-
-        def quant(c):
-            codes = cpool.tile([P, 1024], U32, tag="codes", align_bytes=64)
-            scl = cpool.tile([P, 1024], U8, tag="scl", align_bytes=64)
-            cds[c] = (codes, scl)
-            nc.vector.quantize_mx(out=codes[:].bitcast(FP8X4), scales=scl[:], in_=gts[c][:])
-
-        def mx(c):
-            codes, scl = cds[c]
+        def mx(i):
+            t, h0, nh = units[i]
+            codes, scl = cds[i]
             acc = accp.tile([P, 512], F32, tag="acc")
-            accs[c] = acc
-            for j in range(4):
-                h = 4 * (c % 2) + j
+            accs[i] = acc
+            for j in range(nh):
+                h = h0 + j
                 for gp in range(2):
                     xs = slice(256 * j + 128 * gp, 256 * j + 128 * (gp + 1))
                     ws = slice(128 * (2 * h + gp), 128 * (2 * h + gp + 1))
@@ -182,44 +166,162 @@ def tile_implicitrelationencoder_pb_kernel(tc, out_t, out_w, out_b, self_feat, v
                         stop=(gp == 1),
                     )
 
-        def epi1(c):
-            t = c // 2
-            cols = slice(512 * (c % 2), 512 * (c % 2 + 1))
-            rs = res[t // 3][:, t % 3, cols]
-            nc.vector.tensor_tensor(out=rs, in0=accs[c][:], in1=rs, op=ADD)
+        for i in range(2):
+            op("pe", "bmm%d" % i, ["bias"], lambda i=i: bias_mm(i))
+        for n in range(NB):
+            if n >= TP_BUFS:
+                slot = "C%d" % (n - TP_BUFS)
+            elif n >= TP_BUFS - 2:
+                slot = "bcp%d" % (n - TP_BUFS + 2)
+            else:
+                slot = None
+            op("pe", "TB%d" % n, ["x%d" % unit_of_bank[n], slot], lambda n=n: tb(n))
+            for i in range(NU):
+                if min(last_bank[i] + TP_BUFS, NB - 1) == n:
+                    op(
+                        "pe",
+                        "MX%d" % i,
+                        ["Q%d" % i, "Qw%d" % (units[i][1] // 4), "E1_%d" % (i - ACC_BUFS) if i >= ACC_BUFS else None],
+                        lambda i=i: mx(i),
+                    )
 
-        def epi2(c):
-            t = c // 2
-            cols = slice(512 * (c % 2), 512 * (c % 2 + 1))
+        def bias_copy(i):
+            nc.scalar.copy(out=bias_bc[:, 512 * i : 512 * (i + 1)], in_=tps["b%d" % i][:])
+
+        def regroup_w(b):
+            if b % 8 == 0:
+                wg = gpool.tile([P, 4096], BF16, tag="g", align_bytes=64)
+                gts["w%d" % (b // 8)] = wg
+            nc.scalar.copy(
+                out=gts["w%d" % (b // 8)][:, 512 * (b % 8) : 512 * (b % 8 + 1)].rearrange(
+                    "p (c i t) -> p c t i", i=4, t=4
+                ),
+                in_=xt["w"][:, 512 * b : 512 * (b + 1)].rearrange("p (t c i) -> p c t i", t=4, i=4),
+            )
+
+        def cp(n):
+            i = unit_of_bank[n]
+            j = n - first_bank[i]
+            if j == 0:
+                g = gpool.tile([P, 4096], BF16, tag="g", align_bytes=64)
+                gts[i] = g
+            gw = gts[i][:].bitcast(F32)
+            nc.scalar.copy(
+                out=gw[:, 512 * j : 512 * (j + 1)].rearrange("p (g r u) -> p g r u", g=2, u=2),
+                in_=tps[n][:].rearrange("p (g u) r -> p g r u", u=2),
+            )
+
+        for i in range(2):
+            op("act", "bcp%d" % i, ["bmm%d" % i], lambda i=i: bias_copy(i))
+        for b in range(16):
+            op("act", "R%d" % b, ["w%d" % (b // 8)], lambda b=b: regroup_w(b))
+        g_users = ["Qw0", "Qw1"] + ["Q%d" % i for i in range(NU)]
+        for n in range(NB):
+            i = unit_of_bank[n]
+            slot = None
+            if n == first_bank[i] and i + 2 >= G_BUFS:
+                slot = g_users[i + 2 - G_BUFS]
+            op("act", "C%d" % n, ["TB%d" % n, slot], lambda n=n: cp(n))
+
+        def e0(t):
+            nc.vector.tensor_tensor(
+                out=res[t // 3][:, t % 3, :], in0=self_sb[t // 3][:, t % 3, :], in1=bias_bc[:], op=ADD
+            )
+
+        def quant_w(a):
+            nc.vector.quantize_mx(
+                out=wcodes[:, 1024 * a : 1024 * (a + 1)].bitcast(FP8X4),
+                scales=wscl[:, 1024 * a : 1024 * (a + 1)],
+                in_=gts["w%d" % a][:],
+            )
+
+        def quant(i):
+            nh = units[i][2]
+            codes = cpool.tile([P, 1024], U32, tag="codes", align_bytes=64)
+            scl = cpool.tile([P, 1024], U8, tag="scl", align_bytes=64)
+            cds[i] = (codes, scl)
+            nc.vector.quantize_mx(
+                out=codes[:, : 256 * nh].bitcast(FP8X4), scales=scl[:, : 256 * nh], in_=gts[i][:, : 1024 * nh]
+            )
+
+        def e1(i):
+            t, h0, nh = units[i]
+            rs = res[t // 3][:, t % 3, DH * h0 : DH * (h0 + nh)]
+            nc.vector.tensor_tensor(out=rs, in0=accs[i][:, : DH * nh], in1=rs, op=ADD)
+
+        def e2(i):
+            t, h0, nh = units[i]
+            cols = slice(DH * h0, DH * (h0 + nh))
             rs = res[t // 3][:, t % 3, cols]
             nc.vector.scalar_tensor_tensor(
                 out=rs, in0=rs, scalar=0.0, in1=vis_sb[t // 3][:, t % 3, cols], op0=MAX, op1=ADD
             )
 
-        for n in range(NB + 6):
-            if n < NB:
-                tb(n)
-                if n % 8 == 7:
-                    t = n // 8 + 5
-                    if t < T:
-                        load_x(t, 2 if t == T - 1 else 1)
-                        if t == 6:
-                            load_vis(2)
-            if n >= 5 and (n - 5) % 4 == 0 and 0 <= (n - 5) // 4 - 1 < NCH:
-                mx((n - 5) // 4 - 1)
-            if 0 <= n - 2 < NB:
-                cp(n - 2)
-            if n >= 5 and (n - 5) % 4 == 0:
-                c = (n - 5) // 4
-                if 0 <= c - 1 < NCH:
-                    epi1(c - 1)
-                if c < NCH:
-                    quant(c)
-                if 0 <= c - 1 < NCH:
-                    epi2(c - 1)
+        def q_e0(t):
+            op("dve", "E0_%d" % t, ["self%d" % (t // 3), "bcp1"], lambda: e0(t))
 
-        nc.sync.dma_start(out=o_v[:, 0:3, :], in_=res[0][:])
-        nc.sync.dma_start(out=o_v[:, 3:6, :], in_=res[1][:])
-        nc.sync.dma_start(out=o_v[:, 6:8, :], in_=res[2][:, 0:2, :])
-        nc.sync.dma_start(out=o_v[:, 8, 0:512], in_=res[2][:, 2, 0:512])
-        nc.sync.dma_start(out=o_v[:, 8, 512:1024], in_=res[2][:, 2, 512:1024])
+        def q_qw(a):
+            op("dve", "Qw%d" % a, ["R%d" % (8 * a + 7)], lambda: quant_w(a))
+
+        def q_q(i):
+            op(
+                "dve",
+                "Q%d" % i,
+                ["C%d" % last_bank[i], "MX%d" % (i - C_BUFS) if i >= C_BUFS else None],
+                lambda: quant(i),
+            )
+
+        def q_e1(i):
+            if i >= 0:
+                op("dve", "E1_%d" % i, ["MX%d" % i, "E0_%d" % units[i][0]], lambda: e1(i))
+
+        def q_e2(i):
+            if i >= 0:
+                op("dve", "E2_%d" % i, ["E1_%d" % i, "vis%d" % (units[i][0] // 3)], lambda: e2(i))
+
+        for t in range(3):
+            q_e0(t)
+        q_qw(0)
+        for t in range(3, 6):
+            q_e0(t)
+        q_qw(1)
+        for t in range(6, 9):
+            q_e0(t)
+        for i in range(NU):
+            q_q(i)
+            q_e1(i - 1)
+            q_e2(i - 2)
+        q_e2(NU - 2)
+        q_e1(NU - 1)
+        q_e2(NU - 1)
+
+        def store_tiles(t0, t1):
+            nc.sync.dma_start(out=o_v[:, t0:t1, :], in_=res[t0 // 3][:, t0 % 3 : t0 % 3 + t1 - t0, :])
+
+        def store_unit(i):
+            t, h0, nh = units[i]
+            cols = slice(DH * h0, DH * (h0 + nh))
+            nc.sync.dma_start(out=o_v[:, t, cols], in_=res[t // 3][:, t % 3, cols])
+
+        def last_unit(t):
+            return max(i for i in range(NU) if units[i][0] == t)
+
+        for t0, t1 in ((0, 3), (3, 6), (6, 7), (7, 8)):
+            op("sync", "S%d" % t0, ["E2_%d" % last_unit(t1 - 1)], lambda t0=t0, t1=t1: store_tiles(t0, t1))
+        for i in range(NU):
+            if units[i][0] == T - 1:
+                op("sync", "SU%d" % i, ["E2_%d" % i], lambda i=i: store_unit(i))
+
+        done = set()
+        heads = {"sync": 0, "pe": 0, "act": 0, "dve": 0}
+        moved = True
+        while moved:
+            moved = False
+            for q in ("sync", "pe", "act", "dve"):
+                while heads[q] < len(queues[q]) and all(x in done for x in queues[q][heads[q]][1]):
+                    name, needs, emit = queues[q][heads[q]]
+                    emit()
+                    done.add(name)
+                    heads[q] += 1
+                    moved = True
+        assert all(heads[q] == len(queues[q]) for q in heads)

@@ -64,7 +64,6 @@ def tile_implicitrelationencoder_pb_kernel(tc, out_t, out_w, out_b, self_feat, v
         cpool = ctx.enter_context(tc.tile_pool(name="cpool", bufs=C_BUFS))
         tpp = ctx.enter_context(tc.psum_pool(name="tpp", bufs=TP_BUFS))
         accp = ctx.enter_context(tc.psum_pool(name="accp", bufs=ACC_BUFS))
-        ctx.enter_context(tc.manual_schedule())
 
         brow = const.tile([P, D], BF16)
         ones = const.tile([P, P], BF16)

@@ -64,6 +64,7 @@ def tile_implicitrelationencoder_pb_kernel(tc, out_t, out_w, out_b, self_feat, v
         cpool = ctx.enter_context(tc.tile_pool(name="cpool", bufs=C_BUFS))
         tpp = ctx.enter_context(tc.psum_pool(name="tpp", bufs=TP_BUFS))
         accp = ctx.enter_context(tc.psum_pool(name="accp", bufs=ACC_BUFS))
+        ctx.enter_context(tc.manual_schedule())
 
         brow = const.tile([P, D], BF16)
         ones = const.tile([P, P], BF16)
@@ -85,13 +86,13 @@ def tile_implicitrelationencoder_pb_kernel(tc, out_t, out_w, out_b, self_feat, v
         cds = {}
         accs = {}
 
-        def load_w(a):
-            if a == 0:
+        def load_w(h):
+            if h == 0:
                 wraw = xpool.tile([P, H * K], BF16, tag="x")
                 xt["w"] = wraw
             nc.sync.dma_start(
-                out=xt["w"][:, 4096 * a : 4096 * (a + 1)].rearrange("p (b f) -> p b f", f=256),
-                in_=w_v[:, 16 * a : 16 * (a + 1), :],
+                out=xt["w"][:, K * h : K * (h + 1)].rearrange("p (b f) -> p b f", f=256),
+                in_=w_v[:, 4 * h : 4 * (h + 1), :],
             )
 
         def load_bias():
@@ -121,10 +122,12 @@ def tile_implicitrelationencoder_pb_kernel(tc, out_t, out_w, out_b, self_feat, v
                 if units[i][0] == t:
                     op("sync", "x%d" % i, [slot], lambda i=i: load_x(i))
 
-        op("sync", "w0", [], lambda: load_w(0))
+        for h in range(4):
+            op("sync", "w%d" % h, [], lambda h=h: load_w(h))
         op("sync", "bias", [], load_bias)
         op("sync", "self0", [], lambda: load_self(0))
-        op("sync", "w1", [], lambda: load_w(1))
+        for h in range(4, H):
+            op("sync", "w%d" % h, [], lambda h=h: load_w(h))
         op("sync", "self1", [], lambda: load_self(1))
         op("sync", "self2", [], lambda: load_self(2))
         for t in range(T):
@@ -213,7 +216,7 @@ def tile_implicitrelationencoder_pb_kernel(tc, out_t, out_w, out_b, self_feat, v
         for i in range(2):
             op("act", "bcp%d" % i, ["bmm%d" % i], lambda i=i: bias_copy(i))
         for b in range(16):
-            op("act", "R%d" % b, ["w%d" % (b // 8)], lambda b=b: regroup_w(b))
+            op("act", "R%d" % b, ["w%d" % (b // 2)], lambda b=b: regroup_w(b))
         g_users = ["Qw0", "Qw1"] + ["Q%d" % i for i in range(NU)]
         for n in range(NB):
             i = unit_of_bank[n]

@@ -25,6 +25,8 @@ ACC_BUFS = 2
 G_BUFS = 3
 C_BUFS = 3
 X_BUFS = 6
+WHOLE = 5
+VIS_AFTER = [2, 4, 7]
 
 FLOPS = 2 * ROWS * H * K * DH
 
@@ -86,13 +88,13 @@ def tile_implicitrelationencoder_pb_kernel(tc, out_t, out_w, out_b, self_feat, v
         cds = {}
         accs = {}
 
-        def load_w(h):
-            if h == 0:
+        def load_w(a):
+            if a == 0:
                 wraw = xpool.tile([P, H * K], BF16, tag="x")
                 xt["w"] = wraw
             nc.sync.dma_start(
-                out=xt["w"][:, K * h : K * (h + 1)].rearrange("p (b f) -> p b f", f=256),
-                in_=w_v[:, 4 * h : 4 * (h + 1), :],
+                out=xt["w"][:, 4096 * a : 4096 * (a + 1)].rearrange("p (b f) -> p b f", f=256),
+                in_=w_v[:, 16 * a : 16 * (a + 1), :],
             )
 
         def load_bias():
@@ -104,12 +106,13 @@ def tile_implicitrelationencoder_pb_kernel(tc, out_t, out_w, out_b, self_feat, v
         def load_vis(i):
             nc.sync.dma_start(out=vis_sb[i][:], in_=v_v[:, 3 * i : 3 * i + 3, :])
 
-        def load_x(i):
-            t, h0, nh = units[i]
+        def load_x(t, h0, nh):
             if h0 == 0:
                 xtile = xpool.tile([P, H * K], BF16, tag="x")
                 xt[t] = xtile
             nc.sync.dma_start(out=xt[t][:, K * h0 : K * (h0 + nh)], in_=x_v[:, t, K * h0 : K * (h0 + nh)])
+
+        load_of_unit = {}
 
         def queue_x(t):
             if t < X_BUFS - 1:
@@ -118,22 +121,26 @@ def tile_implicitrelationencoder_pb_kernel(tc, out_t, out_w, out_b, self_feat, v
                 slot = "R15"
             else:
                 slot = "TB%d" % (H * (t - X_BUFS) + H - 1)
+            if t < WHOLE:
+                op("sync", "xt%d" % t, [slot], lambda: load_x(t, 0, H))
             for i in range(NU):
                 if units[i][0] == t:
-                    op("sync", "x%d" % i, [slot], lambda i=i: load_x(i))
+                    if t < WHOLE:
+                        load_of_unit[i] = "xt%d" % t
+                    else:
+                        load_of_unit[i] = "x%d" % i
+                        op("sync", "x%d" % i, [slot], lambda i=i: load_x(t, units[i][1], units[i][2]))
 
-        for h in range(4):
-            op("sync", "w%d" % h, [], lambda h=h: load_w(h))
+        op("sync", "w0", [], lambda: load_w(0))
         op("sync", "bias", [], load_bias)
         op("sync", "self0", [], lambda: load_self(0))
-        for h in range(4, H):
-            op("sync", "w%d" % h, [], lambda h=h: load_w(h))
+        op("sync", "w1", [], lambda: load_w(1))
         op("sync", "self1", [], lambda: load_self(1))
         op("sync", "self2", [], lambda: load_self(2))
         for t in range(T):
             queue_x(t)
-            if t % 3 == 1:
-                op("sync", "vis%d" % (t // 3), [], lambda i=t // 3: load_vis(i))
+            if t in VIS_AFTER:
+                op("sync", "vis%d" % VIS_AFTER.index(t), [], lambda i=VIS_AFTER.index(t): load_vis(i))
 
         def bias_mm(i):
             bp = tpp.tile([P, 512], F32, tag="tp")
@@ -177,7 +184,7 @@ def tile_implicitrelationencoder_pb_kernel(tc, out_t, out_w, out_b, self_feat, v
                 slot = "bcp%d" % (n - TP_BUFS + 2)
             else:
                 slot = None
-            op("pe", "TB%d" % n, ["x%d" % unit_of_bank[n], slot], lambda n=n: tb(n))
+            op("pe", "TB%d" % n, [load_of_unit[unit_of_bank[n]], slot], lambda n=n: tb(n))
             for i in range(NU):
                 if min(last_bank[i] + TP_BUFS, NB - 1) == n:
                     op(
@@ -216,7 +223,7 @@ def tile_implicitrelationencoder_pb_kernel(tc, out_t, out_w, out_b, self_feat, v
         for i in range(2):
             op("act", "bcp%d" % i, ["bmm%d" % i], lambda i=i: bias_copy(i))
         for b in range(16):
-            op("act", "R%d" % b, ["w%d" % (b // 2)], lambda b=b: regroup_w(b))
+            op("act", "R%d" % b, ["w%d" % (b // 8)], lambda b=b: regroup_w(b))
         g_users = ["Qw0", "Qw1"] + ["Q%d" % i for i in range(NU)]
         for n in range(NB):
             i = unit_of_bank[n]

from contextlib import ExitStack

import concourse.mybir as mybir
from concourse.masks import make_identity

BF16 = mybir.dt.bfloat16
F32 = mybir.dt.float32
U32 = mybir.dt.uint32
U8 = mybir.dt.uint8
FP8X4 = mybir.dt.float8_e4m3fn_x4
ADD = mybir.AluOpType.add
MAX = mybir.AluOpType.max

P = 128
ROWS = 32 * 36
T = ROWS // P
H = 8
K = 1024
DH = 128
D = H * DH
NB = T * H

TP_BUFS = 6
ACC_BUFS = 2
G_BUFS = 3
C_BUFS = 3
X_BUFS = 6
WHOLE = 5
VIS_AFTER = [2, 4, 7]

FLOPS = 2 * ROWS * H * K * DH


def tile_implicitrelationencoder_pb_kernel(tc, out_t, out_w, out_b, self_feat, vis, out):
    nc = tc.nc
    x_v = out_t.rearrange("b n h k -> (b n) (h k)").rearrange("(p t) f -> p t f", t=T)
    w_v = out_w.rearrange("h (s q e) c -> q (h s) (e c)", q=P, e=2)
    s_v = self_feat.rearrange("b n d -> (b n) d").rearrange("(p t) d -> p t d", t=T)
    v_v = vis.rearrange("b n d -> (b n) d").rearrange("(p t) d -> p t d", t=T)
    o_v = out.rearrange("b n d -> (b n) d").rearrange("(p t) d -> p t d", t=T)

    units = []
    for t in range(T):
        sizes = [2, 2, 2, 2] if t == T - 1 else [4, 4]
        h0 = 0
        for nh in sizes:
            units.append((t, h0, nh))
            h0 += nh
    NU = len(units)
    first_bank = [H * t + h0 for (t, h0, nh) in units]
    last_bank = [H * t + h0 + nh - 1 for (t, h0, nh) in units]
    unit_of_bank = {}
    for i in range(NU):
        for n in range(first_bank[i], last_bank[i] + 1):
            unit_of_bank[n] = i

    queues = {"sync": [], "pe": [], "act": [], "dve": []}

    def op(queue, name, needs, emit):
        queues[queue].append((name, [x for x in needs if x is not None], emit))

    with ExitStack() as ctx:
        const = ctx.enter_context(tc.tile_pool(name="const", bufs=1))
        xpool = ctx.enter_context(tc.tile_pool(name="xpool", bufs=X_BUFS))
        gpool = ctx.enter_context(tc.tile_pool(name="gpool", bufs=G_BUFS))
        cpool = ctx.enter_context(tc.tile_pool(name="cpool", bufs=C_BUFS))
        tpp = ctx.enter_context(tc.psum_pool(name="tpp", bufs=TP_BUFS))
        accp = ctx.enter_context(tc.psum_pool(name="accp", bufs=ACC_BUFS))
        ctx.enter_context(tc.manual_schedule())

        brow = const.tile([P, D], BF16)
        ones = const.tile([P, P], BF16)
        ident = const.tile([P, P], F32)
        bias_bc = const.tile([P, D], F32)
        wcodes = const.tile([P, 2 * H * DH], U32, align_bytes=64)
        wscl = const.tile([P, 2 * H * DH], U8, align_bytes=64)
        self_sb = [const.tile([P, 3, D], BF16, name="self%d" % i) for i in range(3)]
        vis_sb = [const.tile([P, 3, D], BF16, name="vis%d" % i) for i in range(3)]
        res = [const.tile([P, 3, D], F32, name="res%d" % i) for i in range(3)]

        nc.gpsimd.memset(brow[:], 0.0)
        nc.gpsimd.memset(ones[:], 1.0)
        make_identity(nc, ident[:])

        xt = {}
        tps = {}
        gts = {}
        cds = {}
        accs = {}

        def load_w(a):
            if a == 0:
                wraw = xpool.tile([P, H * K], BF16, tag="x")
                xt["w"] = wraw
            nc.sync.dma_start(
                out=xt["w"][:, 4096 * a : 4096 * (a + 1)].rearrange("p (b f) -> p b f", f=256),
                in_=w_v[:, 16 * a : 16 * (a + 1), :],
            )

        def load_bias():
            nc.sync.dma_start(out=brow[0:1, :], in_=out_b.rearrange("(o d) -> o d", o=1))

        def load_self(i):
            nc.sync.dma_start(out=self_sb[i][:], in_=s_v[:, 3 * i : 3 * i + 3, :])

        def load_vis(i):
            nc.sync.dma_start(out=vis_sb[i][:], in_=v_v[:, 3 * i : 3 * i + 3, :])

        def load_x(t, h0, nh):
            if h0 == 0:
                xtile = xpool.tile([P, H * K], BF16, tag="x")
                xt[t] = xtile
            nc.sync.dma_start(out=xt[t][:, K * h0 : K * (h0 + nh)], in_=x_v[:, t, K * h0 : K * (h0 + nh)])

        load_of_unit = {}

        def queue_x(t):
            if t < X_BUFS - 1:
                slot = None
            elif t == X_BUFS - 1:
                slot = "R15"
            else:
                slot = "TB%d" % (H * (t - X_BUFS) + H - 1)
            if t < WHOLE:
                op("sync", "xt%d" % t, [slot], lambda: load_x(t, 0, H))
            for i in range(NU):
                if units[i][0] == t:
                    if t < WHOLE:
                        load_of_unit[i] = "xt%d" % t
                    else:
                        load_of_unit[i] = "x%d" % i
                        op("sync", "x%d" % i, [slot], lambda i=i: load_x(t, units[i][1], units[i][2]))

        op("sync", "w0", [], lambda: load_w(0))
        op("sync", "bias", [], load_bias)
        op("sync", "self0", [], lambda: load_self(0))
        op("sync", "w1", [], lambda: load_w(1))
        op("sync", "self1", [], lambda: load_self(1))
        op("sync", "self2", [], lambda: load_self(2))
        for t in range(T):
            queue_x(t)
            if t in VIS_AFTER:
                op("sync", "vis%d" % VIS_AFTER.index(t), [], lambda i=VIS_AFTER.index(t): load_vis(i))

        def bias_mm(i):
            bp = tpp.tile([P, 512], F32, tag="tp")
            tps["b%d" % i] = bp
            nc.tensor.matmul(bp[:], lhsT=ones[:], rhs=brow[:, 512 * i : 512 * (i + 1)], start=True, stop=True)

        def tb(n):
            xw = xt[n // H][:].bitcast(F32)
            hh = n % H
            tp = tpp.tile([P, 4, P], F32, tag="tp")
            tps[n] = tp
            for u in range(4):
                nc.tensor.transpose(tp[:, u, :], xw[:, 512 * hh + 128 * u : 512 * hh + 128 * (u + 1)], ident[:])

        def mx(i):
            t, h0, nh = units[i]
            codes, scl = cds[i]
            acc = accp.tile([P, 512], F32, tag="acc")
            accs[i] = acc
            for j in range(nh):
                h = h0 + j
                for gp in range(2):
                    xs = slice(256 * j + 128 * gp, 256 * j + 128 * (gp + 1))
                    ws = slice(128 * (2 * h + gp), 128 * (2 * h + gp + 1))
                    nc.tensor.matmul_mx(
                        out=acc[:, 128 * j : 128 * (j + 1)],
                        lhsT=codes[:, xs].bitcast(FP8X4),
                        lhsT_scale=scl[:, xs],
                        rhs=wcodes[:, ws].bitcast(FP8X4),
                        rhs_scale=wscl[:, ws],
                        start=(gp == 0),
                        stop=(gp == 1),
                    )

        for i in range(2):
            op("pe", "bmm%d" % i, ["bias"], lambda i=i: bias_mm(i))
        for n in range(NB):
            if n >= TP_BUFS:
                slot = "C%d" % (n - TP_BUFS)
            elif n >= TP_BUFS - 2:
                slot = "bcp%d" % (n - TP_BUFS + 2)
            else:
                slot = None
            op("pe", "TB%d" % n, [load_of_unit[unit_of_bank[n]], slot], lambda n=n: tb(n))
            for i in range(NU):
                if min(last_bank[i] + TP_BUFS, NB - 1) == n:
                    op(
                        "pe",
                        "MX%d" % i,
                        ["Q%d" % i, "Qw%d" % (units[i][1] // 4), "E1_%d" % (i - ACC_BUFS) if i >= ACC_BUFS else None],
                        lambda i=i: mx(i),
                    )

        def bias_copy(i):
            nc.scalar.copy(out=bias_bc[:, 512 * i : 512 * (i + 1)], in_=tps["b%d" % i][:])

        def regroup_w(b):
            if b % 8 == 0:
                wg = gpool.tile([P, 4096], BF16, tag="g", align_bytes=64)
                gts["w%d" % (b // 8)] = wg
            nc.scalar.copy(
                out=gts["w%d" % (b // 8)][:, 512 * (b % 8) : 512 * (b % 8 + 1)].rearrange(
                    "p (c i t) -> p c t i", i=4, t=4
                ),
                in_=xt["w"][:, 512 * b : 512 * (b + 1)].rearrange("p (t c i) -> p c t i", t=4, i=4),
            )

        def cp(n):
            i = unit_of_bank[n]
            j = n - first_bank[i]
            if j == 0:
                g = gpool.tile([P, 4096], BF16, tag="g", align_bytes=64)
                gts[i] = g
            gw = gts[i][:].bitcast(F32)
            nc.scalar.copy(
                out=gw[:, 512 * j : 512 * (j + 1)].rearrange("p (g r u) -> p g r u", g=2, u=2),
                in_=tps[n][:].rearrange("p (g u) r -> p g r u", u=2),
            )

        for i in range(2):
            op("act", "bcp%d" % i, ["bmm%d" % i], lambda i=i: bias_copy(i))
        for b in range(16):
            op("act", "R%d" % b, ["w%d" % (b // 8)], lambda b=b: regroup_w(b))
        g_users = ["Qw0", "Qw1"] + ["Q%d" % i for i in range(NU)]
        for n in range(NB):
            i = unit_of_bank[n]
            slot = None
            if n == first_bank[i] and i + 2 >= G_BUFS:
                slot = g_users[i + 2 - G_BUFS]
            op("act", "C%d" % n, ["TB%d" % n, slot], lambda n=n: cp(n))

        def e0(t):
            nc.vector.tensor_tensor(
                out=res[t // 3][:, t % 3, :], in0=self_sb[t // 3][:, t % 3, :], in1=bias_bc[:], op=ADD
            )

        def quant_w(a):
            nc.vector.quantize_mx(
                out=wcodes[:, 1024 * a : 1024 * (a + 1)].bitcast(FP8X4),
                scales=wscl[:, 1024 * a : 1024 * (a + 1)],
                in_=gts["w%d" % a][:],
            )

        def quant(i):
            nh = units[i][2]
            codes = cpool.tile([P, 1024], U32, tag="codes", align_bytes=64)
            scl = cpool.tile([P, 1024], U8, tag="scl", align_bytes=64)
            cds[i] = (codes, scl)
            nc.vector.quantize_mx(
                out=codes[:, : 256 * nh].bitcast(FP8X4), scales=scl[:, : 256 * nh], in_=gts[i][:, : 1024 * nh]
            )

        def e1(i):
            t, h0, nh = units[i]
            rs = res[t // 3][:, t % 3, DH * h0 : DH * (h0 + nh)]
            nc.vector.tensor_tensor(out=rs, in0=accs[i][:, : DH * nh], in1=rs, op=ADD)

        def e2(i):
            t, h0, nh = units[i]
            cols = slice(DH * h0, DH * (h0 + nh))
            rs = res[t // 3][:, t % 3, cols]
            nc.vector.scalar_tensor_tensor(
                out=rs, in0=rs, scalar=0.0, in1=vis_sb[t // 3][:, t % 3, cols], op0=MAX, op1=ADD
            )

        def q_e0(t):
            op("dve", "E0_%d" % t, ["self%d" % (t // 3), "bcp1"], lambda: e0(t))

        def q_qw(a):
            op("dve", "Qw%d" % a, ["R%d" % (8 * a + 7)], lambda: quant_w(a))

        def q_q(i):
            op(
                "dve",
                "Q%d" % i,
                ["C%d" % last_bank[i], "MX%d" % (i - C_BUFS) if i >= C_BUFS else None],
                lambda: quant(i),
            )

        def q_e1(i):
            if i >= 0:
                op("dve", "E1_%d" % i, ["MX%d" % i, "E0_%d" % units[i][0]], lambda: e1(i))

        def q_e2(i):
            if i >= 0:
                op("dve", "E2_%d" % i, ["E1_%d" % i, "vis%d" % (units[i][0] // 3)], lambda: e2(i))

        for t in range(3):
            q_e0(t)
        q_qw(0)
        for t in range(3, 6):
            q_e0(t)
        q_qw(1)
        for t in range(6, 9):
            q_e0(t)
        for i in range(NU):
            q_q(i)
            q_e1(i - 1)
            q_e2(i - 2)
        q_e2(NU - 2)
        q_e1(NU - 1)
        q_e2(NU - 1)

        def store_tiles(t0, t1):
            nc.sync.dma_start(out=o_v[:, t0:t1, :], in_=res[t0 // 3][:, t0 % 3 : t0 % 3 + t1 - t0, :])

        def store_unit(i):
            t, h0, nh = units[i]
            cols = slice(DH * h0, DH * (h0 + nh))
            nc.sync.dma_start(out=o_v[:, t, cols], in_=res[t // 3][:, t % 3, cols])

        def last_unit(t):
            return max(i for i in range(NU) if units[i][0] == t)

        for t0, t1 in ((0, 3), (3, 6), (6, 7), (7, 8)):
            op("sync", "S%d" % t0, ["E2_%d" % last_unit(t1 - 1)], lambda t0=t0, t1=t1: store_tiles(t0, t1))
        for i in range(NU):
            if units[i][0] == T - 1:
                op("sync", "SU%d" % i, ["E2_%d" % i], lambda i=i: store_unit(i))

        done = set()
        heads = {"sync": 0, "pe": 0, "act": 0, "dve": 0}
        moved = True
        while moved:
            moved = False
            for q in ("sync", "pe", "act", "dve"):
                while heads[q] < len(queues[q]) and all(x in done for x in queues[q][heads[q]][1]):
                    name, needs, emit = queues[q][heads[q]]
                    emit()
                    done.add(name)
                    heads[q] += 1
                    moved = True
        assert all(heads[q] == len(queues[q]) for q in heads)
